import numpy as np
import ml_dtypes


def mxq(x, axis, fmt="e4m3"):
    dtype, down = {"e4m3": (ml_dtypes.float8_e4m3fn, 7), "e5m2": (ml_dtypes.float8_e5m2, 14)}[fmt]
    v = np.moveaxis(np.asarray(x, np.float32).astype(ml_dtypes.bfloat16).astype(np.float64), axis, -1)
    blocks = v.reshape(v.shape[:-1] + (-1, 32))
    amax = np.abs(blocks).max(-1, keepdims=True)
    byte = np.maximum(np.where(amax > 0, np.frexp(amax)[1] - 1 + 127, 0) - down, 1)
    scale = np.exp2(byte - 127.0)
    codes = (blocks / scale).astype(np.float32).astype(dtype).astype(np.float64)
    return np.moveaxis((codes * scale).reshape(v.shape), -1, axis)


WIDE = False


def mx_kscale(k):
    if not WIDE:
        return np.ones(k)
    levels = np.array([10, -10, 5, -5, 0])
    a = np.random.permutation(np.resize(levels, k // 512 * 4)).reshape(k // 512, 4)
    idx = np.arange(k)
    return np.exp2(a[idx // 512, idx % 128 // 32])


BF16 = ml_dtypes.bfloat16


def bf(x):
    return np.asarray(x, np.float32).astype(BF16)


def f64(x):
    return np.asarray(x).astype(np.float64)


E2M1 = np.array([0.0, 0.5, 1.0, 1.5, 2.0, 3.0, 4.0, 6.0, -0.0, -0.5, -1.0, -1.5, -2.0, -3.0, -4.0, -6.0])


def pack_weight(w, fmt):
    k, n = w.shape
    w = f64(bf(w)).reshape(k // 32, 32, n)
    amax = np.abs(w).max(1)
    if fmt == "e4m3":
        byte = np.frexp(amax)[1] - 1 + 127 - 7
    else:
        mant, ex = np.frexp(amax / 6.0)
        byte = np.where(mant > 0.5, ex, ex - 1) + 127
    byte = np.clip(np.where(amax > 0, byte, 1), 1, 254)
    scaled = (w * np.exp2(127.0 - byte)[:, None, :]).reshape(k, n).astype(np.float32)
    by_word = np.ascontiguousarray(scaled.reshape(k // 512, 128, 4, n).transpose(0, 1, 3, 2))
    if fmt == "e4m3":
        words = by_word.astype(ml_dtypes.float8_e4m3fn).view(np.uint8)
    else:
        c = by_word.astype(ml_dtypes.float4_e2m1fn).view(np.uint8) & 0xF
        words = c[..., 0::2] | (c[..., 1::2] << 4)
    return np.ascontiguousarray(words), np.ascontiguousarray(byte.astype(np.uint8).reshape(k // 512, 16, n))


def unpack_weight(words, scales, fmt):
    g, p, n, _ = words.shape
    if fmt == "e4m3":
        vals = np.ascontiguousarray(words).view(ml_dtypes.float8_e4m3fn).astype(np.float64)
    else:
        nib = np.empty((g, p, n, 4), np.uint8)
        nib[..., 0::2] = words & 0xF
        nib[..., 1::2] = words >> 4
        vals = E2M1[nib]
    vals = vals * np.repeat(np.exp2(scales.astype(np.float64) - 127.0), 8, axis=1)[..., None]
    return vals.transpose(0, 1, 3, 2).reshape(g * 512, n)

def pack4(w):
    words, scales = pack_weight(w, "e2m1")
    return words.reshape(words.shape[0], 128, -1), scales


def unpack4(words, scales):
    return unpack_weight(words.reshape(words.shape[0], 128, -1, 2), scales, "e2m1")


B, S, D, NH, NKV, HD, QB = 2, 2048, 1024, 4, 2, 128, 512
Q_DIM = NH * HD
KV_DIM = NKV * HD


def rot(t, f0, f1):
    tp = t.reshape(t.shape[:-1] + (HD // 2, 2))
    t0, t1 = tp[..., 0], tp[..., 1]
    row1 = t0 * f0 + t1 * f1
    row0 = t0 * f1 - t1 * f0
    return np.stack([row0, row1], axis=-1).reshape(t.shape)


def setup_inputs():
    s = mx_kscale(D)
    x = bf(np.random.standard_normal((B, S, D)) * s)
    freqs_cis = bf(np.random.standard_normal((S, HD)))
    w = np.random.standard_normal((Q_DIM + 2 * KV_DIM, D)) / np.sqrt(D) / s
    words, scales = pack4(np.ascontiguousarray(w.T))
    return {"x": x,
            "freqs_cis": freqs_cis,
            "Wqkv_words": words,
            "Wqkv_scales": scales}


def reference(x, freqs_cis, Wqkv_words, Wqkv_scales):
    xqkv = mxq(f64(x), 2, "e4m3") @ unpack4(Wqkv_words, Wqkv_scales)
    xq = xqkv[..., :Q_DIM].reshape(B, S, NH, HD)
    xk = xqkv[..., Q_DIM:Q_DIM + KV_DIM].reshape(B, S, NKV, HD)
    xv = xqkv[..., Q_DIM + KV_DIM:].reshape(B, S, NKV, HD)
    f = f64(freqs_cis).reshape(S, 1, HD // 2, 2)
    f0, f1 = f[..., 0], f[..., 1]
    q_rot = rot(xq, f0, f1).transpose(0, 2, 1, 3)
    k_rot = rot(xk, f0, f1).transpose(0, 2, 1, 3)
    v = xv.transpose(0, 2, 1, 3)
    return q_rot, k_rot, v

@@ -1,0 +1,202 @@
+from contextlib import ExitStack
+
+import concourse.mybir as mybir
+from concourse.masks import make_identity
+
+F32 = mybir.dt.float32
+BF16 = mybir.dt.bfloat16
+I32 = mybir.dt.int32
+U32 = mybir.dt.uint32
+U8 = mybir.dt.uint8
+FP8X4 = mybir.dt.float8_e4m3fn_x4
+FP4X4 = mybir.dt.float4_e2m1fn_x4
+MULT = mybir.AluOpType.mult
+ADD = mybir.AluOpType.add
+
+P = 128
+PACK = 4
+K_PASS = P * PACK
+BATCH, SEQ, D_IN = 2, 2048, 1024
+PASSES = D_IN // K_PASS
+HEAD = 128
+PAIRS = HEAD // 2
+Q_HEADS, K_HEADS, V_HEADS = 4, 2, 2
+ROTATED = Q_HEADS + K_HEADS
+HEADS = ROTATED + V_HEADS
+N_BANK = 512
+ROWS = 4
+CHUNK = P * ROWS
+SEQ_CHUNKS = SEQ // CHUNK
+N_CHUNKS = BATCH * SEQ_CHUNKS
+N_TILES = N_CHUNKS * ROWS
+WORDS = K_PASS // 2
+
+BUNCH = 4
+BUNCH_AT = 1
+AHEAD = 3
+
+FLOPS = 2 * BATCH * SEQ * D_IN * HEADS * HEAD
+
+
+def tile_rlaattention_pa_t_kernel(
+    tc, x, freqs_cis, Wqkv_words, Wqkv_scales, out_0, out_1, out_2
+):
+    nc = tc.nc
+    with ExitStack() as ctx:
+        consts = ctx.enter_context(tc.tile_pool(name="consts", bufs=1))
+        x_pool = ctx.enter_context(tc.tile_pool(name="x_pool", bufs=N_CHUNKS))
+        grouped_pool = ctx.enter_context(tc.tile_pool(name="grouped_pool", bufs=2 * BUNCH))
+        codes_pool = ctx.enter_context(tc.tile_pool(name="codes_pool", bufs=2 * AHEAD))
+        prod_pool = ctx.enter_context(tc.tile_pool(name="prod_pool", bufs=3))
+        out_pool = ctx.enter_context(tc.tile_pool(name="out_pool", bufs=3))
+        xt_psum = ctx.enter_context(tc.psum_pool(name="xt_psum", bufs=BUNCH))
+        acc_psum = ctx.enter_context(tc.psum_pool(name="acc_psum", bufs=2))
+        ctx.enter_context(tc.manual_schedule())
+
+        ident = consts.tile([P, P], F32, name="ident")
+        make_identity(nc, ident[:])
+
+        w_words = consts.tile([P, PASSES, 2 * HEADS * HEAD], U8, name="w_words", align_bytes=64)
+        w_scales = consts.tile([P, PASSES, HEADS * HEAD], U8, name="w_scales", align_bytes=64)
+        nc.vector.memset(w_scales[:].bitcast(I32), 0)
+
+        freqs = consts.tile([P, SEQ_CHUNKS, ROWS * PAIRS, 2], BF16, name="freqs")
+        even_factor = consts.tile([P, SEQ_CHUNKS, ROWS * PAIRS, 2], BF16, name="even_factor")
+        odd_factor = consts.tile([P, SEQ_CHUNKS, ROWS * PAIRS, 2], BF16, name="odd_factor")
+
+        x_chunks = []
+        for c in range(N_CHUNKS):
+            b, m = divmod(c, SEQ_CHUNKS)
+            if b == 0:
+                nc.sync.dma_start(
+                    out=freqs[:, m].rearrange("p n e -> p (n e)"),
+                    in_=freqs_cis.rearrange("(m p r) f -> m p (r f)", p=P, r=ROWS)[m],
+                )
+            x_sb = x_pool.tile([P, ROWS, D_IN], BF16, name="x_sb")
+            nc.sync.dma_start(
+                out=x_sb[:].rearrange("p r d -> p (r d)"),
+                in_=x[b].rearrange("(m p r) d -> m p (r d)", p=P, r=ROWS)[m],
+            )
+            x_chunks.append(x_sb)
+            if c == 0:
+                for quadrant in range(4):
+                    nc.sync.dma_start(
+                        out=w_scales[32 * quadrant : 32 * quadrant + 4].bitcast(I32),
+                        in_=Wqkv_scales.bitcast(I32)[
+                            :, 4 * quadrant : 4 * quadrant + 4, :
+                        ].rearrange("g r n -> r g n"),
+                    )
+                nc.sync.dma_start(
+                    out=w_words[:].bitcast(I32),
+                    in_=Wqkv_words.bitcast(I32).rearrange("g p n -> p g n"),
+                )
+
+        grouped_tiles = {}
+        code_tiles = {}
+        out_tiles = {}
+
+        def build_factors(m):
+            f0 = freqs[:, m, :, 0]
+            f1 = freqs[:, m, :, 1]
+            nc.scalar.copy(out=even_factor[:, m, :, 0], in_=f1)
+            nc.scalar.copy(out=even_factor[:, m, :, 1], in_=f0)
+            nc.scalar.mul(out=odd_factor[:, m, :, 0], in_=f0, mul=-1.0)
+            nc.scalar.copy(out=odd_factor[:, m, :, 1], in_=f1)
+
+        def transpose_tile(i):
+            c, r = divmod(i, ROWS)
+            words = x_chunks[c][:].bitcast(F32)
+            xt = xt_psum.tile([P, PASSES, 2, P], F32, name="xt")
+            for g in range(PASSES):
+                for u in range(2):
+                    nc.tensor.transpose(
+                        xt[:, g, u, :], words[:, r, WORDS * g + u : WORDS * (g + 1) : 2], ident[:]
+                    )
+            grouped = grouped_pool.tile([P, PASSES, P, PACK], BF16, name="grouped", align_bytes=64)
+            nc.scalar.copy(
+                out=grouped[:].bitcast(F32), in_=xt[:].rearrange("p g u t -> p g t u")
+            )
+            grouped_tiles[i] = grouped
+
+        def quantise_tile(i):
+            x_codes = codes_pool.tile([P, PASSES, P], U32, name="x_codes", align_bytes=64)
+            x_scales = codes_pool.tile([P, PASSES, P], U8, name="x_scales", align_bytes=64)
+            nc.vector.quantize_mx(
+                out=x_codes[:].rearrange("p g t -> p (g t)").bitcast(FP8X4),
+                scales=x_scales[:].rearrange("p g t -> p (g t)"),
+                in_=grouped_tiles.pop(i)[:].rearrange("p g t j -> p (g t j)"),
+            )
+            code_tiles[i] = (x_codes, x_scales)
+
+        def project_tile(i):
+            x_codes, x_scales = code_tiles.pop(i)
+            acc_q = acc_psum.tile([P, N_BANK], F32, name="acc_q")
+            acc_kv = acc_psum.tile([P, N_BANK], F32, name="acc_kv")
+            for half, acc in enumerate((acc_q, acc_kv)):
+                for g in range(PASSES):
+                    nc.tensor.matmul_mx(
+                        out=acc[:],
+                        lhsT=x_codes[:, g, :].bitcast(FP8X4),
+                        lhsT_scale=x_scales[:, g, :],
+                        rhs=w_words[:, g, 2 * N_BANK * half : 2 * N_BANK * (half + 1)].bitcast(FP4X4),
+                        rhs_scale=w_scales[:, g, N_BANK * half : N_BANK * (half + 1)],
+                        start=(g == 0),
+                        stop=(g == PASSES - 1),
+                    )
+            return acc_q, acc_kv
+
+        def rotate_tile(i, acc_q, acc_kv):
+            c, r = divmod(i, ROWS)
+            m = c % SEQ_CHUNKS
+            if r == 0:
+                out_tiles[c] = out_pool.tile([P, HEADS, ROWS, HEAD], F32, name="out_sb")
+            out_sb = out_tiles[c]
+            even = prod_pool.tile([P, ROTATED, HEAD], F32, name="even")
+            odd = prod_pool.tile([P, ROTATED, HEAD], F32, name="odd")
+            pairs = slice(PAIRS * r, PAIRS * (r + 1))
+            for acc, first, heads in ((acc_q, 0, Q_HEADS), (acc_kv, Q_HEADS, K_HEADS)):
+                t = acc[:, : heads * HEAD].rearrange("p (h j e) -> p h j e", h=heads, e=2)
+                shape = [P, heads, PAIRS, 2]
+                for e, (prod, factor) in enumerate(((even, even_factor), (odd, odd_factor))):
+                    nc.vector.tensor_tensor(
+                        out=prod[:, first : first + heads, :].rearrange("p h (j e) -> p h j e", e=2),
+                        in0=t[:, :, :, e : e + 1].to_broadcast(shape),
+                        in1=factor[:, m, pairs, :].unsqueeze(1).to_broadcast(shape),
+                        op=MULT,
+                    )
+            nc.scalar.copy(
+                out=out_sb[:, ROTATED:, r, :],
+                in_=acc_kv[:, K_HEADS * HEAD :].rearrange("p (h f) -> p h f", h=V_HEADS),
+            )
+            nc.gpsimd.tensor_tensor(out=out_sb[:, :ROTATED, r, :], in0=even[:], in1=odd[:], op=ADD)
+
+        def store_chunk(c):
+            b, m = divmod(c, SEQ_CHUNKS)
+            out_sb = out_tiles.pop(c)
+            first = 0
+            for dram, heads in ((out_0, Q_HEADS), (out_1, K_HEADS), (out_2, V_HEADS)):
+                nc.sync.dma_start(
+                    out=dram[b].rearrange("h (m p r) f -> m p h (r f)", p=P, r=ROWS)[m],
+                    in_=out_sb[:, first : first + heads].rearrange("p h r f -> p h (r f)"),
+                )
+                first += heads
+
+        build_factors(0)
+        for i in range(BUNCH):
+            transpose_tile(i)
+        for i in range(AHEAD):
+            quantise_tile(i)
+        for i in range(N_TILES):
+            c, r = divmod(i, ROWS)
+            banks = project_tile(i)
+            if r == 0 and c + 1 < SEQ_CHUNKS:
+                build_factors(c + 1)
+            next_bunch = (i // BUNCH + 1) * BUNCH
+            if i % BUNCH == BUNCH_AT and next_bunch < N_TILES:
+                for j in range(next_bunch, next_bunch + BUNCH):
+                    transpose_tile(j)
+            rotate_tile(i, *banks)
+            if i + AHEAD < N_TILES:
+                quantise_tile(i + AHEAD)
+            if r == ROWS - 1:
+                store_chunk(c)

@@ -34,6 +34,8 @@ WORDS = K_PASS // 2
 BUNCH = 4
 BUNCH_AT = 1
 AHEAD = 3
+BY_TILE = N_TILES - ROWS
+PAIR = 2
 
 FLOPS = 2 * BATCH * SEQ * D_IN * HEADS * HEAD
 
@@ -47,6 +49,7 @@ def tile_rlaattention_pa_t_kernel(
         x_pool = ctx.enter_context(tc.tile_pool(name="x_pool", bufs=N_CHUNKS))
         grouped_pool = ctx.enter_context(tc.tile_pool(name="grouped_pool", bufs=2 * BUNCH))
         codes_pool = ctx.enter_context(tc.tile_pool(name="codes_pool", bufs=2 * AHEAD))
+        last_pool = ctx.enter_context(tc.tile_pool(name="last_pool", bufs=ROWS // PAIR))
         prod_pool = ctx.enter_context(tc.tile_pool(name="prod_pool", bufs=3))
         out_pool = ctx.enter_context(tc.tile_pool(name="out_pool", bufs=3))
         xt_psum = ctx.enter_context(tc.psum_pool(name="xt_psum", bufs=BUNCH))
@@ -93,6 +96,8 @@ def tile_rlaattention_pa_t_kernel(
 
         grouped_tiles = {}
         code_tiles = {}
+        pair_tiles = {}
+        pair_codes = {}
         out_tiles = {}
 
         def build_factors(m):
@@ -112,11 +117,18 @@ def tile_rlaattention_pa_t_kernel(
                     nc.tensor.transpose(
                         xt[:, g, u, :], words[:, r, WORDS * g + u : WORDS * (g + 1) : 2], ident[:]
                     )
-            grouped = grouped_pool.tile([P, PASSES, P, PACK], BF16, name="grouped", align_bytes=64)
-            nc.scalar.copy(
-                out=grouped[:].bitcast(F32), in_=xt[:].rearrange("p g u t -> p g t u")
-            )
-            grouped_tiles[i] = grouped
+            if i < BY_TILE:
+                grouped = grouped_pool.tile([P, PASSES, P, PACK], BF16, name="grouped", align_bytes=64)
+                grouped_tiles[i] = grouped
+                target = grouped[:]
+            else:
+                k, member = divmod(i - BY_TILE, PAIR)
+                if member == 0:
+                    pair_tiles[k] = last_pool.tile(
+                        [P, PAIR, PASSES, P, PACK], BF16, name="grouped_pair", align_bytes=64
+                    )
+                target = pair_tiles[k][:, member]
+            nc.scalar.copy(out=target.bitcast(F32), in_=xt[:].rearrange("p g u t -> p g t u"))
 
         def quantise_tile(i):
             x_codes = codes_pool.tile([P, PASSES, P], U32, name="x_codes", align_bytes=64)
@@ -127,6 +139,16 @@ def tile_rlaattention_pa_t_kernel(
                 in_=grouped_tiles.pop(i)[:].rearrange("p g t j -> p (g t j)"),
             )
             code_tiles[i] = (x_codes, x_scales)
+
+        def quantise_pair(k):
+            x_codes = last_pool.tile([P, PAIR, PASSES, P], U32, name="pair_codes", align_bytes=64)
+            x_scales = last_pool.tile([P, PAIR, PASSES, P], U8, name="pair_scales", align_bytes=64)
+            nc.vector.quantize_mx(
+                out=x_codes[:].rearrange("p i g t -> p (i g t)").bitcast(FP8X4),
+                scales=x_scales[:].rearrange("p i g t -> p (i g t)"),
+                in_=pair_tiles.pop(k)[:].rearrange("p i g t j -> p (i g t j)"),
+            )
+            pair_codes[k] = (x_codes, x_scales)
 
         def project_tile(i):
             x_codes, x_scales = code_tiles.pop(i)
@@ -170,23 +192,90 @@ def tile_rlaattention_pa_t_kernel(
             )
             nc.gpsimd.tensor_tensor(out=out_sb[:, :ROTATED, r, :], in0=even[:], in1=odd[:], op=ADD)
 
-        def store_chunk(c):
+        def store_heads(c, dram, first, in_dram, heads):
             b, m = divmod(c, SEQ_CHUNKS)
-            out_sb = out_tiles.pop(c)
-            first = 0
-            for dram, heads in ((out_0, Q_HEADS), (out_1, K_HEADS), (out_2, V_HEADS)):
-                nc.sync.dma_start(
-                    out=dram[b].rearrange("h (m p r) f -> m p h (r f)", p=P, r=ROWS)[m],
-                    in_=out_sb[:, first : first + heads].rearrange("p h r f -> p h (r f)"),
+            nc.sync.dma_start(
+                out=dram[b, in_dram : in_dram + heads].rearrange(
+                    "h (m p r) f -> m p h (r f)", p=P, r=ROWS
+                )[m],
+                in_=out_tiles[c][:, first : first + heads].rearrange("p h r f -> p h (r f)"),
+            )
+
+        def store_chunk(c):
+            store_heads(c, out_2, ROTATED, 0, V_HEADS)
+            store_heads(c, out_1, Q_HEADS, 0, K_HEADS)
+            store_heads(c, out_0, 0, 0, Q_HEADS)
+
+        def project_heads(heads, banks):
+            for r in range(ROWS):
+                x_codes, x_scales = pair_codes[r // PAIR]
+                for g in range(PASSES):
+                    for h, bank in zip(heads, banks):
+                        nc.tensor.matmul_mx(
+                            out=bank[:, r, :],
+                            lhsT=x_codes[:, r % PAIR, g, :].bitcast(FP8X4),
+                            lhsT_scale=x_scales[:, r % PAIR, g, :],
+                            rhs=w_words[:, g, 2 * HEAD * h : 2 * HEAD * (h + 1)].bitcast(FP4X4),
+                            rhs_scale=w_scales[:, g, HEAD * h : HEAD * (h + 1)],
+                            start=(g == 0),
+                            stop=(g == PASSES - 1),
+                        )
+
+        def head_products(c, bank):
+            m = c % SEQ_CHUNKS
+            t = bank[:].rearrange("p r (j e) -> p (r j) e", e=2)
+            shape = [P, ROWS * PAIRS, 2]
+            even = prod_pool.tile([P, ROWS * PAIRS, 2], F32, name="even")
+            odd = prod_pool.tile([P, ROWS * PAIRS, 2], F32, name="odd")
+            for e, (prod, factor) in enumerate(((even, even_factor), (odd, odd_factor))):
+                nc.vector.tensor_tensor(
+                    out=prod[:], in0=t[:, :, e : e + 1].to_broadcast(shape), in1=factor[:, m], op=MULT
                 )
-                first += heads
+            return even, odd
+
+        def head_sum(engine, c, h, even, odd):
+            engine.tensor_tensor(
+                out=out_tiles[c][:, h].rearrange("p r (j e) -> p (r j) e", e=2),
+                in0=even[:],
+                in1=odd[:],
+                op=ADD,
+            )
+
+        def last_chunk(c):
+            out_tiles[c] = out_pool.tile([P, HEADS, ROWS, HEAD], F32, name="out_sb")
+            bank_shape = [P, ROWS, HEAD]
+            k_banks = [xt_psum.tile(bank_shape, F32, name="xt") for h in range(K_HEADS)]
+            project_heads(range(Q_HEADS, ROTATED), k_banks)
+            v_banks = [xt_psum.tile(bank_shape, F32, name="xt") for h in range(V_HEADS)]
+            project_heads(range(ROTATED, HEADS), v_banks)
+            q_banks = []
+            for first in range(0, Q_HEADS, 2):
+                two = [
+                    acc_psum.tile(bank_shape, F32, name="acc_q"),
+                    acc_psum.tile(bank_shape, F32, name="acc_kv"),
+                ]
+                project_heads(range(first, first + 2), two)
+                q_banks.extend(two)
+            for h, bank in enumerate(v_banks):
+                nc.scalar.copy(out=out_tiles[c][:, ROTATED + h], in_=bank[:])
+            store_heads(c, out_2, ROTATED, 0, V_HEADS)
+            for h, bank in zip(range(Q_HEADS, ROTATED), k_banks):
+                head_sum(nc.gpsimd, c, h, *head_products(c, bank))
+                store_heads(c, out_1, h, h - Q_HEADS, 1)
+            for h in range(2):
+                head_sum(nc.gpsimd, c, h, *head_products(c, q_banks[h]))
+                store_heads(c, out_0, h, h, 1)
+            left = [(h, head_products(c, q_banks[h])) for h in range(2, Q_HEADS)]
+            for h, (even, odd) in left:
+                head_sum(nc.vector, c, h, even, odd)
+                store_heads(c, out_0, h, h, 1)
 
         build_factors(0)
         for i in range(BUNCH):
             transpose_tile(i)
         for i in range(AHEAD):
             quantise_tile(i)
-        for i in range(N_TILES):
+        for i in range(BY_TILE):
             c, r = divmod(i, ROWS)
             banks = project_tile(i)
             if r == 0 and c + 1 < SEQ_CHUNKS:
@@ -196,7 +285,10 @@ def tile_rlaattention_pa_t_kernel(
                 for j in range(next_bunch, next_bunch + BUNCH):
                     transpose_tile(j)
             rotate_tile(i, *banks)
-            if i + AHEAD < N_TILES:
+            if i + AHEAD < BY_TILE:
                 quantise_tile(i + AHEAD)
+            elif i + AHEAD - BY_TILE < ROWS // PAIR:
+                quantise_pair(i + AHEAD - BY_TILE)
             if r == ROWS - 1:
                 store_chunk(c)
+        last_chunk(N_CHUNKS - 1)

@@ -64,8 +64,7 @@ def tile_rlaattention_pa_t_kernel(
         nc.vector.memset(w_scales[:].bitcast(I32), 0)
 
         freqs = consts.tile([P, SEQ_CHUNKS, ROWS * PAIRS, 2], BF16, name="freqs")
-        even_factor = consts.tile([P, SEQ_CHUNKS, ROWS * PAIRS, 2], BF16, name="even_factor")
-        odd_factor = consts.tile([P, SEQ_CHUNKS, ROWS * PAIRS, 2], BF16, name="odd_factor")
+        factors = consts.tile([P, SEQ_CHUNKS, 2, ROWS * PAIRS, 2], BF16, name="factors")
 
         x_chunks = []
         for c in range(N_CHUNKS):
@@ -103,10 +102,10 @@ def tile_rlaattention_pa_t_kernel(
         def build_factors(m):
             f0 = freqs[:, m, :, 0]
             f1 = freqs[:, m, :, 1]
-            nc.scalar.copy(out=even_factor[:, m, :, 0], in_=f1)
-            nc.scalar.copy(out=even_factor[:, m, :, 1], in_=f0)
-            nc.scalar.mul(out=odd_factor[:, m, :, 0], in_=f0, mul=-1.0)
-            nc.scalar.copy(out=odd_factor[:, m, :, 1], in_=f1)
+            nc.scalar.copy(out=factors[:, m, 0, :, 0], in_=f1)
+            nc.scalar.copy(out=factors[:, m, 0, :, 1], in_=f0)
+            nc.scalar.mul(out=factors[:, m, 1, :, 0], in_=f0, mul=-1.0)
+            nc.scalar.copy(out=factors[:, m, 1, :, 1], in_=f1)
 
         def transpose_tile(i):
             c, r = divmod(i, ROWS)
@@ -173,24 +172,24 @@ def tile_rlaattention_pa_t_kernel(
             if r == 0:
                 out_tiles[c] = out_pool.tile([P, HEADS, ROWS, HEAD], F32, name="out_sb")
             out_sb = out_tiles[c]
-            even = prod_pool.tile([P, ROTATED, HEAD], F32, name="even")
-            odd = prod_pool.tile([P, ROTATED, HEAD], F32, name="odd")
+            prod = prod_pool.tile([P, 2, ROTATED, HEAD], F32, name="prod")
             pairs = slice(PAIRS * r, PAIRS * (r + 1))
             for acc, first, heads in ((acc_q, 0, Q_HEADS), (acc_kv, Q_HEADS, K_HEADS)):
-                t = acc[:, : heads * HEAD].rearrange("p (h j e) -> p h j e", h=heads, e=2)
-                shape = [P, heads, PAIRS, 2]
-                for e, (prod, factor) in enumerate(((even, even_factor), (odd, odd_factor))):
-                    nc.vector.tensor_tensor(
-                        out=prod[:, first : first + heads, :].rearrange("p h (j e) -> p h j e", e=2),
-                        in0=t[:, :, :, e : e + 1].to_broadcast(shape),
-                        in1=factor[:, m, pairs, :].unsqueeze(1).to_broadcast(shape),
-                        op=MULT,
-                    )
+                shape = [P, 2, heads, PAIRS, 2]
+                nc.vector.tensor_tensor(
+                    out=prod[:, :, first : first + heads, :].rearrange("p t h (j e) -> p t h j e", e=2),
+                    in0=acc[:, : heads * HEAD]
+                    .rearrange("p (h j t) -> p t h j", h=heads, t=2)
+                    .unsqueeze(4)
+                    .to_broadcast(shape),
+                    in1=factors[:, m, :, pairs, :].unsqueeze(2).to_broadcast(shape),
+                    op=MULT,
+                )
             nc.scalar.copy(
                 out=out_sb[:, ROTATED:, r, :],
                 in_=acc_kv[:, K_HEADS * HEAD :].rearrange("p (h f) -> p h f", h=V_HEADS),
             )
-            nc.gpsimd.tensor_tensor(out=out_sb[:, :ROTATED, r, :], in0=even[:], in1=odd[:], op=ADD)
+            nc.gpsimd.tensor_tensor(out=out_sb[:, :ROTATED, r, :], in0=prod[:, 0], in1=prod[:, 1], op=ADD)
 
         def store_heads(c, dram, first, in_dram, heads):
             b, m = divmod(c, SEQ_CHUNKS)
@@ -223,21 +222,21 @@ def tile_rlaattention_pa_t_kernel(
 
         def head_products(c, bank):
             m = c % SEQ_CHUNKS
-            t = bank[:].rearrange("p r (j e) -> p (r j) e", e=2)
-            shape = [P, ROWS * PAIRS, 2]
-            even = prod_pool.tile([P, ROWS * PAIRS, 2], F32, name="even")
-            odd = prod_pool.tile([P, ROWS * PAIRS, 2], F32, name="odd")
-            for e, (prod, factor) in enumerate(((even, even_factor), (odd, odd_factor))):
-                nc.vector.tensor_tensor(
-                    out=prod[:], in0=t[:, :, e : e + 1].to_broadcast(shape), in1=factor[:, m], op=MULT
-                )
-            return even, odd
+            shape = [P, 2, ROWS * PAIRS, 2]
+            prod = prod_pool.tile(shape, F32, name="prod")
+            nc.vector.tensor_tensor(
+                out=prod[:],
+                in0=bank[:].rearrange("p r (j t) -> p t (r j)", t=2).unsqueeze(3).to_broadcast(shape),
+                in1=factors[:, m],
+                op=MULT,
+            )
+            return prod
 
-        def head_sum(engine, c, h, even, odd):
+        def head_sum(engine, c, h, prod):
             engine.tensor_tensor(
                 out=out_tiles[c][:, h].rearrange("p r (j e) -> p (r j) e", e=2),
-                in0=even[:],
-                in1=odd[:],
+                in0=prod[:, 0],
+                in1=prod[:, 1],
                 op=ADD,
             )
 
@@ -260,14 +259,14 @@ def tile_rlaattention_pa_t_kernel(
                 nc.scalar.copy(out=out_tiles[c][:, ROTATED + h], in_=bank[:])
             store_heads(c, out_2, ROTATED, 0, V_HEADS)
             for h, bank in zip(range(Q_HEADS, ROTATED), k_banks):
-                head_sum(nc.gpsimd, c, h, *head_products(c, bank))
+                head_sum(nc.gpsimd, c, h, head_products(c, bank))
                 store_heads(c, out_1, h, h - Q_HEADS, 1)
             for h in range(2):
-                head_sum(nc.gpsimd, c, h, *head_products(c, q_banks[h]))
+                head_sum(nc.gpsimd, c, h, head_products(c, q_banks[h]))
                 store_heads(c, out_0, h, h, 1)
             left = [(h, head_products(c, q_banks[h])) for h in range(2, Q_HEADS)]
-            for h, (even, odd) in left:
-                head_sum(nc.vector, c, h, even, odd)
+            for h, prod in left:
+                head_sum(nc.vector, c, h, prod)
                 store_heads(c, out_0, h, h, 1)
 
         build_factors(0)

@@ -35,7 +35,7 @@ BUNCH = 4
 BUNCH_AT = 1
 AHEAD = 3
 BY_TILE = N_TILES - ROWS
-PAIR = 2
+PAIR = 4
 
 FLOPS = 2 * BATCH * SEQ * D_IN * HEADS * HEAD
 
@@ -50,7 +50,7 @@ def tile_rlaattention_pa_t_kernel(
         grouped_pool = ctx.enter_context(tc.tile_pool(name="grouped_pool", bufs=2 * BUNCH))
         codes_pool = ctx.enter_context(tc.tile_pool(name="codes_pool", bufs=2 * AHEAD))
         last_pool = ctx.enter_context(tc.tile_pool(name="last_pool", bufs=ROWS // PAIR))
-        prod_pool = ctx.enter_context(tc.tile_pool(name="prod_pool", bufs=3))
+        prod_pool = ctx.enter_context(tc.tile_pool(name="prod_pool", bufs=4))
         out_pool = ctx.enter_context(tc.tile_pool(name="out_pool", bufs=3))
         xt_psum = ctx.enter_context(tc.psum_pool(name="xt_psum", bufs=BUNCH))
         acc_psum = ctx.enter_context(tc.psum_pool(name="acc_psum", bufs=2))
@@ -202,6 +202,8 @@ def tile_rlaattention_pa_t_kernel(
 
         def store_chunk(c):
             store_heads(c, out_2, ROTATED, 0, V_HEADS)
+            if c == N_CHUNKS - 2:
+                last_values(c + 1)
             store_heads(c, out_1, Q_HEADS, 0, K_HEADS)
             store_heads(c, out_0, 0, 0, Q_HEADS)
 
@@ -240,13 +242,19 @@ def tile_rlaattention_pa_t_kernel(
                 op=ADD,
             )
 
-        def last_chunk(c):
+        bank_shape = [P, ROWS, HEAD]
+
+        def last_values(c):
             out_tiles[c] = out_pool.tile([P, HEADS, ROWS, HEAD], F32, name="out_sb")
-            bank_shape = [P, ROWS, HEAD]
-            k_banks = [xt_psum.tile(bank_shape, F32, name="xt") for h in range(K_HEADS)]
-            project_heads(range(Q_HEADS, ROTATED), k_banks)
             v_banks = [xt_psum.tile(bank_shape, F32, name="xt") for h in range(V_HEADS)]
             project_heads(range(ROTATED, HEADS), v_banks)
+            for h, bank in enumerate(v_banks):
+                nc.scalar.copy(out=out_tiles[c][:, ROTATED + h], in_=bank[:])
+            store_heads(c, out_2, ROTATED, 0, V_HEADS)
+
+        def last_rotated(c):
+            k_banks = [xt_psum.tile(bank_shape, F32, name="xt") for h in range(K_HEADS)]
+            project_heads(range(Q_HEADS, ROTATED), k_banks)
             q_banks = []
             for first in range(0, Q_HEADS, 2):
                 two = [
@@ -255,16 +263,12 @@ def tile_rlaattention_pa_t_kernel(
                 ]
                 project_heads(range(first, first + 2), two)
                 q_banks.extend(two)
-            for h, bank in enumerate(v_banks):
-                nc.scalar.copy(out=out_tiles[c][:, ROTATED + h], in_=bank[:])
-            store_heads(c, out_2, ROTATED, 0, V_HEADS)
             for h, bank in zip(range(Q_HEADS, ROTATED), k_banks):
                 head_sum(nc.gpsimd, c, h, head_products(c, bank))
                 store_heads(c, out_1, h, h - Q_HEADS, 1)
-            for h in range(2):
-                head_sum(nc.gpsimd, c, h, head_products(c, q_banks[h]))
-                store_heads(c, out_0, h, h, 1)
-            left = [(h, head_products(c, q_banks[h])) for h in range(2, Q_HEADS)]
+            head_sum(nc.gpsimd, c, 0, head_products(c, q_banks[0]))
+            store_heads(c, out_0, 0, 0, 1)
+            left = [(h, head_products(c, q_banks[h])) for h in range(1, Q_HEADS)]
             for h, prod in left:
                 head_sum(nc.vector, c, h, prod)
                 store_heads(c, out_0, h, h, 1)
@@ -280,7 +284,8 @@ def tile_rlaattention_pa_t_kernel(
             if r == 0 and c + 1 < SEQ_CHUNKS:
                 build_factors(c + 1)
             next_bunch = (i // BUNCH + 1) * BUNCH
-            if i % BUNCH == BUNCH_AT and next_bunch < N_TILES:
+            bunch_at = BUNCH_AT if next_bunch < BY_TILE else BUNCH_AT - 1
+            if i % BUNCH == bunch_at and next_bunch < N_TILES:
                 for j in range(next_bunch, next_bunch + BUNCH):
                     transpose_tile(j)
             rotate_tile(i, *banks)
@@ -290,4 +295,4 @@ def tile_rlaattention_pa_t_kernel(
                 quantise_pair(i + AHEAD - BY_TILE)
             if r == ROWS - 1:
                 store_chunk(c)
-        last_chunk(N_CHUNKS - 1)
+        last_rotated(N_CHUNKS - 1)

@@ -37,6 +37,8 @@ AHEAD = 3
 BY_TILE = N_TILES - ROWS
 PAIR = 4
 
+WARM_UP = 12
+
 FLOPS = 2 * BATCH * SEQ * D_IN * HEADS * HEAD
 
 
@@ -62,6 +64,14 @@ def tile_rlaattention_pa_t_kernel(
         w_words = consts.tile([P, PASSES, 2 * HEADS * HEAD], U8, name="w_words", align_bytes=64)
         w_scales = consts.tile([P, PASSES, HEADS * HEAD], U8, name="w_scales", align_bytes=64)
         nc.vector.memset(w_scales[:].bitcast(I32), 0)
+
+        zeros = consts.tile([P, P + N_BANK], BF16, name="zeros")
+        nc.vector.memset(zeros[:], 0.0)
+        unread = acc_psum.tile([P, N_BANK], F32, name="acc_q")
+        for i in range(WARM_UP):
+            nc.tensor.matmul(
+                out=unread[:], lhsT=zeros[:, :P], rhs=zeros[:, P:], start=True, stop=True
+            )
 
         freqs = consts.tile([P, SEQ_CHUNKS, ROWS * PAIRS, 2], BF16, name="freqs")
         factors = consts.tile([P, SEQ_CHUNKS, 2, ROWS * PAIRS, 2], BF16, name="factors")

@@ -37,7 +37,7 @@ AHEAD = 3
 BY_TILE = N_TILES - ROWS
 PAIR = 4
 
-WARM_UP = 12
+WARM_UP = 10
 
 FLOPS = 2 * BATCH * SEQ * D_IN * HEADS * HEAD
 
@@ -58,20 +58,20 @@ def tile_rlaattention_pa_t_kernel(
         acc_psum = ctx.enter_context(tc.psum_pool(name="acc_psum", bufs=2))
         ctx.enter_context(tc.manual_schedule())
 
+        zeros = consts.tile([P, P + N_BANK], BF16, name="zeros")
+        nc.gpsimd.memset(zeros[:], 0.0)
+        unread = acc_psum.tile([P, N_BANK], F32, name="acc_q")
+        for i in range(WARM_UP):
+            nc.tensor.matmul(
+                out=unread[:], lhsT=zeros[:, :P], rhs=zeros[:, P:], start=True, stop=True
+            )
+
         ident = consts.tile([P, P], F32, name="ident")
         make_identity(nc, ident[:])
 
         w_words = consts.tile([P, PASSES, 2 * HEADS * HEAD], U8, name="w_words", align_bytes=64)
         w_scales = consts.tile([P, PASSES, HEADS * HEAD], U8, name="w_scales", align_bytes=64)
         nc.vector.memset(w_scales[:].bitcast(I32), 0)
-
-        zeros = consts.tile([P, P + N_BANK], BF16, name="zeros")
-        nc.vector.memset(zeros[:], 0.0)
-        unread = acc_psum.tile([P, N_BANK], F32, name="acc_q")
-        for i in range(WARM_UP):
-            nc.tensor.matmul(
-                out=unread[:], lhsT=zeros[:, :P], rhs=zeros[:, P:], start=True, stop=True
-            )
 
         freqs = consts.tile([P, SEQ_CHUNKS, ROWS * PAIRS, 2], BF16, name="freqs")
         factors = consts.tile([P, SEQ_CHUNKS, 2, ROWS * PAIRS, 2], BF16, name="factors")

@@ -295,7 +295,14 @@ def tile_rlaattention_pa_t_kernel(
                 build_factors(c + 1)
             next_bunch = (i // BUNCH + 1) * BUNCH
             bunch_at = BUNCH_AT if next_bunch < BY_TILE else BUNCH_AT - 1
-            if i % BUNCH == bunch_at and next_bunch < N_TILES:
+            if i < BUNCH:
+                if i % BUNCH == 1:
+                    for j in range(next_bunch, next_bunch + 2):
+                        transpose_tile(j)
+                if i % BUNCH == 3:
+                    for j in range(next_bunch + 2, next_bunch + 4):
+                        transpose_tile(j)
+            elif i % BUNCH == bunch_at and next_bunch < N_TILES:
                 for j in range(next_bunch, next_bunch + BUNCH):
                     transpose_tile(j)
             rotate_tile(i, *banks)

@@ -73,7 +73,6 @@ def tile_rlaattention_pa_t_kernel(
         w_scales = consts.tile([P, PASSES, HEADS * HEAD], U8, name="w_scales", align_bytes=64)
         nc.vector.memset(w_scales[:].bitcast(I32), 0)
 
-        freqs = consts.tile([P, SEQ_CHUNKS, ROWS * PAIRS, 2], BF16, name="freqs")
         factors = consts.tile([P, SEQ_CHUNKS, 2, ROWS * PAIRS, 2], BF16, name="factors")
 
         x_chunks = []
@@ -81,7 +80,7 @@ def tile_rlaattention_pa_t_kernel(
             b, m = divmod(c, SEQ_CHUNKS)
             if b == 0:
                 nc.sync.dma_start(
-                    out=freqs[:, m].rearrange("p n e -> p (n e)"),
+                    out=factors[:, m, 1].rearrange("p n e -> p (n e)"),
                     in_=freqs_cis.rearrange("(m p r) f -> m p (r f)", p=P, r=ROWS)[m],
                 )
             x_sb = x_pool.tile([P, ROWS, D_IN], BF16, name="x_sb")
@@ -110,12 +109,8 @@ def tile_rlaattention_pa_t_kernel(
         out_tiles = {}
 
         def build_factors(m):
-            f0 = freqs[:, m, :, 0]
-            f1 = freqs[:, m, :, 1]
-            nc.scalar.copy(out=factors[:, m, 0, :, 0], in_=f1)
-            nc.scalar.copy(out=factors[:, m, 0, :, 1], in_=f0)
-            nc.scalar.mul(out=factors[:, m, 1, :, 0], in_=f0, mul=-1.0)
-            nc.scalar.copy(out=factors[:, m, 1, :, 1], in_=f1)
+            nc.scalar.copy(out=factors[:, m, 0], in_=factors[:, m, 1, :, ::-1])
+            nc.scalar.mul(out=factors[:, m, 1, :, 0], in_=factors[:, m, 1, :, 0], mul=-1.0)
 
         def transpose_tile(i):
             c, r = divmod(i, ROWS)

from contextlib import ExitStack

import concourse.mybir as mybir
from concourse.masks import make_identity

F32 = mybir.dt.float32
BF16 = mybir.dt.bfloat16
I32 = mybir.dt.int32
U32 = mybir.dt.uint32
U8 = mybir.dt.uint8
FP8X4 = mybir.dt.float8_e4m3fn_x4
FP4X4 = mybir.dt.float4_e2m1fn_x4
MULT = mybir.AluOpType.mult
ADD = mybir.AluOpType.add

P = 128
PACK = 4
K_PASS = P * PACK
BATCH, SEQ, D_IN = 2, 2048, 1024
PASSES = D_IN // K_PASS
HEAD = 128
PAIRS = HEAD // 2
Q_HEADS, K_HEADS, V_HEADS = 4, 2, 2
ROTATED = Q_HEADS + K_HEADS
HEADS = ROTATED + V_HEADS
N_BANK = 512
ROWS = 4
CHUNK = P * ROWS
SEQ_CHUNKS = SEQ // CHUNK
N_CHUNKS = BATCH * SEQ_CHUNKS
N_TILES = N_CHUNKS * ROWS
WORDS = K_PASS // 2

BUNCH = 4
BUNCH_AT = 1
AHEAD = 3
BY_TILE = N_TILES - ROWS
PAIR = 4

WARM_UP = 10

FLOPS = 2 * BATCH * SEQ * D_IN * HEADS * HEAD


def tile_rlaattention_pa_t_kernel(
    tc, x, freqs_cis, Wqkv_words, Wqkv_scales, out_0, out_1, out_2
):
    nc = tc.nc
    with ExitStack() as ctx:
        consts = ctx.enter_context(tc.tile_pool(name="consts", bufs=1))
        x_pool = ctx.enter_context(tc.tile_pool(name="x_pool", bufs=N_CHUNKS))
        grouped_pool = ctx.enter_context(tc.tile_pool(name="grouped_pool", bufs=2 * BUNCH))
        codes_pool = ctx.enter_context(tc.tile_pool(name="codes_pool", bufs=2 * AHEAD))
        last_pool = ctx.enter_context(tc.tile_pool(name="last_pool", bufs=ROWS // PAIR))
        prod_pool = ctx.enter_context(tc.tile_pool(name="prod_pool", bufs=4))
        out_pool = ctx.enter_context(tc.tile_pool(name="out_pool", bufs=3))
        xt_psum = ctx.enter_context(tc.psum_pool(name="xt_psum", bufs=BUNCH))
        acc_psum = ctx.enter_context(tc.psum_pool(name="acc_psum", bufs=2))
        ctx.enter_context(tc.manual_schedule())

        zeros = consts.tile([P, P + N_BANK], BF16, name="zeros")
        nc.gpsimd.memset(zeros[:], 0.0)
        unread = acc_psum.tile([P, N_BANK], F32, name="acc_q")
        for i in range(WARM_UP):
            nc.tensor.matmul(
                out=unread[:], lhsT=zeros[:, :P], rhs=zeros[:, P:], start=True, stop=True
            )

        ident = consts.tile([P, P], F32, name="ident")
        make_identity(nc, ident[:])

        w_words = consts.tile([P, PASSES, 2 * HEADS * HEAD], U8, name="w_words", align_bytes=64)
        w_scales = consts.tile([P, PASSES, HEADS * HEAD], U8, name="w_scales", align_bytes=64)
        nc.vector.memset(w_scales[:].bitcast(I32), 0)

        factors = consts.tile([P, SEQ_CHUNKS, 2, ROWS * PAIRS, 2], BF16, name="factors")

        x_chunks = []
        for c in range(N_CHUNKS):
            b, m = divmod(c, SEQ_CHUNKS)
            if b == 0:
                nc.sync.dma_start(
                    out=factors[:, m, 1].rearrange("p n e -> p (n e)"),
                    in_=freqs_cis.rearrange("(m p r) f -> m p (r f)", p=P, r=ROWS)[m],
                )
            x_sb = x_pool.tile([P, ROWS, D_IN], BF16, name="x_sb")
            nc.sync.dma_start(
                out=x_sb[:].rearrange("p r d -> p (r d)"),
                in_=x[b].rearrange("(m p r) d -> m p (r d)", p=P, r=ROWS)[m],
            )
            x_chunks.append(x_sb)
            if c == 0:
                for quadrant in range(4):
                    nc.sync.dma_start(
                        out=w_scales[32 * quadrant : 32 * quadrant + 4].bitcast(I32),
                        in_=Wqkv_scales.bitcast(I32)[
                            :, 4 * quadrant : 4 * quadrant + 4, :
                        ].rearrange("g r n -> r g n"),
                    )
                nc.sync.dma_start(
                    out=w_words[:].bitcast(I32),
                    in_=Wqkv_words.bitcast(I32).rearrange("g p n -> p g n"),
                )

        grouped_tiles = {}
        code_tiles = {}
        pair_tiles = {}
        pair_codes = {}
        out_tiles = {}

        def build_factors(m):
            nc.scalar.copy(out=factors[:, m, 0], in_=factors[:, m, 1, :, ::-1])
            nc.scalar.mul(out=factors[:, m, 1, :, 0], in_=factors[:, m, 1, :, 0], mul=-1.0)

        def transpose_tile(i):
            c, r = divmod(i, ROWS)
            words = x_chunks[c][:].bitcast(F32)
            xt = xt_psum.tile([P, PASSES, 2, P], F32, name="xt")
            for g in range(PASSES):
                for u in range(2):
                    nc.tensor.transpose(
                        xt[:, g, u, :], words[:, r, WORDS * g + u : WORDS * (g + 1) : 2], ident[:]
                    )
            if i < BY_TILE:
                grouped = grouped_pool.tile([P, PASSES, P, PACK], BF16, name="grouped", align_bytes=64)
                grouped_tiles[i] = grouped
                target = grouped[:]
            else:
                k, member = divmod(i - BY_TILE, PAIR)
                if member == 0:
                    pair_tiles[k] = last_pool.tile(
                        [P, PAIR, PASSES, P, PACK], BF16, name="grouped_pair", align_bytes=64
                    )
                target = pair_tiles[k][:, member]
            nc.scalar.copy(out=target.bitcast(F32), in_=xt[:].rearrange("p g u t -> p g t u"))

        def quantise_tile(i):
            x_codes = codes_pool.tile([P, PASSES, P], U32, name="x_codes", align_bytes=64)
            x_scales = codes_pool.tile([P, PASSES, P], U8, name="x_scales", align_bytes=64)
            nc.vector.quantize_mx(
                out=x_codes[:].rearrange("p g t -> p (g t)").bitcast(FP8X4),
                scales=x_scales[:].rearrange("p g t -> p (g t)"),
                in_=grouped_tiles.pop(i)[:].rearrange("p g t j -> p (g t j)"),
            )
            code_tiles[i] = (x_codes, x_scales)

        def quantise_pair(k):
            x_codes = last_pool.tile([P, PAIR, PASSES, P], U32, name="pair_codes", align_bytes=64)
            x_scales = last_pool.tile([P, PAIR, PASSES, P], U8, name="pair_scales", align_bytes=64)
            nc.vector.quantize_mx(
                out=x_codes[:].rearrange("p i g t -> p (i g t)").bitcast(FP8X4),
                scales=x_scales[:].rearrange("p i g t -> p (i g t)"),
                in_=pair_tiles.pop(k)[:].rearrange("p i g t j -> p (i g t j)"),
            )
            pair_codes[k] = (x_codes, x_scales)

        def project_tile(i):
            x_codes, x_scales = code_tiles.pop(i)
            acc_q = acc_psum.tile([P, N_BANK], F32, name="acc_q")
            acc_kv = acc_psum.tile([P, N_BANK], F32, name="acc_kv")
            for half, acc in enumerate((acc_q, acc_kv)):
                for g in range(PASSES):
                    nc.tensor.matmul_mx(
                        out=acc[:],
                        lhsT=x_codes[:, g, :].bitcast(FP8X4),
                        lhsT_scale=x_scales[:, g, :],
                        rhs=w_words[:, g, 2 * N_BANK * half : 2 * N_BANK * (half + 1)].bitcast(FP4X4),
                        rhs_scale=w_scales[:, g, N_BANK * half : N_BANK * (half + 1)],
                        start=(g == 0),
                        stop=(g == PASSES - 1),
                    )
            return acc_q, acc_kv

        def rotate_tile(i, acc_q, acc_kv):
            c, r = divmod(i, ROWS)
            m = c % SEQ_CHUNKS
            if r == 0:
                out_tiles[c] = out_pool.tile([P, HEADS, ROWS, HEAD], F32, name="out_sb")
            out_sb = out_tiles[c]
            prod = prod_pool.tile([P, 2, ROTATED, HEAD], F32, name="prod")
            pairs = slice(PAIRS * r, PAIRS * (r + 1))
            for acc, first, heads in ((acc_q, 0, Q_HEADS), (acc_kv, Q_HEADS, K_HEADS)):
                shape = [P, 2, heads, PAIRS, 2]
                nc.vector.tensor_tensor(
                    out=prod[:, :, first : first + heads, :].rearrange("p t h (j e) -> p t h j e", e=2),
                    in0=acc[:, : heads * HEAD]
                    .rearrange("p (h j t) -> p t h j", h=heads, t=2)
                    .unsqueeze(4)
                    .to_broadcast(shape),
                    in1=factors[:, m, :, pairs, :].unsqueeze(2).to_broadcast(shape),
                    op=MULT,
                )
            nc.scalar.copy(
                out=out_sb[:, ROTATED:, r, :],
                in_=acc_kv[:, K_HEADS * HEAD :].rearrange("p (h f) -> p h f", h=V_HEADS),
            )
            nc.gpsimd.tensor_tensor(out=out_sb[:, :ROTATED, r, :], in0=prod[:, 0], in1=prod[:, 1], op=ADD)

        def store_heads(c, dram, first, in_dram, heads):
            b, m = divmod(c, SEQ_CHUNKS)
            nc.sync.dma_start(
                out=dram[b, in_dram : in_dram + heads].rearrange(
                    "h (m p r) f -> m p h (r f)", p=P, r=ROWS
                )[m],
                in_=out_tiles[c][:, first : first + heads].rearrange("p h r f -> p h (r f)"),
            )

        def store_chunk(c):
            store_heads(c, out_2, ROTATED, 0, V_HEADS)
            if c == N_CHUNKS - 2:
                last_values(c + 1)
            store_heads(c, out_1, Q_HEADS, 0, K_HEADS)
            store_heads(c, out_0, 0, 0, Q_HEADS)

        def project_heads(heads, banks):
            for r in range(ROWS):
                x_codes, x_scales = pair_codes[r // PAIR]
                for g in range(PASSES):
                    for h, bank in zip(heads, banks):
                        nc.tensor.matmul_mx(
                            out=bank[:, r, :],
                            lhsT=x_codes[:, r % PAIR, g, :].bitcast(FP8X4),
                            lhsT_scale=x_scales[:, r % PAIR, g, :],
                            rhs=w_words[:, g, 2 * HEAD * h : 2 * HEAD * (h + 1)].bitcast(FP4X4),
                            rhs_scale=w_scales[:, g, HEAD * h : HEAD * (h + 1)],
                            start=(g == 0),
                            stop=(g == PASSES - 1),
                        )

        def head_products(c, bank):
            m = c % SEQ_CHUNKS
            shape = [P, 2, ROWS * PAIRS, 2]
            prod = prod_pool.tile(shape, F32, name="prod")
            nc.vector.tensor_tensor(
                out=prod[:],
                in0=bank[:].rearrange("p r (j t) -> p t (r j)", t=2).unsqueeze(3).to_broadcast(shape),
                in1=factors[:, m],
                op=MULT,
            )
            return prod

        def head_sum(engine, c, h, prod):
            engine.tensor_tensor(
                out=out_tiles[c][:, h].rearrange("p r (j e) -> p (r j) e", e=2),
                in0=prod[:, 0],
                in1=prod[:, 1],
                op=ADD,
            )

        bank_shape = [P, ROWS, HEAD]

        def last_values(c):
            out_tiles[c] = out_pool.tile([P, HEADS, ROWS, HEAD], F32, name="out_sb")
            v_banks = [xt_psum.tile(bank_shape, F32, name="xt") for h in range(V_HEADS)]
            project_heads(range(ROTATED, HEADS), v_banks)
            for h, bank in enumerate(v_banks):
                nc.scalar.copy(out=out_tiles[c][:, ROTATED + h], in_=bank[:])
            store_heads(c, out_2, ROTATED, 0, V_HEADS)

        def last_rotated(c):
            k_banks = [xt_psum.tile(bank_shape, F32, name="xt") for h in range(K_HEADS)]
            project_heads(range(Q_HEADS, ROTATED), k_banks)
            q_banks = []
            for first in range(0, Q_HEADS, 2):
                two = [
                    acc_psum.tile(bank_shape, F32, name="acc_q"),
                    acc_psum.tile(bank_shape, F32, name="acc_kv"),
                ]
                project_heads(range(first, first + 2), two)
                q_banks.extend(two)
            for h, bank in zip(range(Q_HEADS, ROTATED), k_banks):
                head_sum(nc.gpsimd, c, h, head_products(c, bank))
                store_heads(c, out_1, h, h - Q_HEADS, 1)
            head_sum(nc.gpsimd, c, 0, head_products(c, q_banks[0]))
            store_heads(c, out_0, 0, 0, 1)
            left = [(h, head_products(c, q_banks[h])) for h in range(1, Q_HEADS)]
            for h, prod in left:
                head_sum(nc.vector, c, h, prod)
                store_heads(c, out_0, h, h, 1)

        build_factors(0)
        for i in range(BUNCH):
            transpose_tile(i)
        for i in range(AHEAD):
            quantise_tile(i)
        for i in range(BY_TILE):
            c, r = divmod(i, ROWS)
            banks = project_tile(i)
            if r == 0 and c + 1 < SEQ_CHUNKS:
                build_factors(c + 1)
            next_bunch = (i // BUNCH + 1) * BUNCH
            bunch_at = BUNCH_AT if next_bunch < BY_TILE else BUNCH_AT - 1
            if i < BUNCH:
                if i % BUNCH == 1:
                    for j in range(next_bunch, next_bunch + 2):
                        transpose_tile(j)
                if i % BUNCH == 3:
                    for j in range(next_bunch + 2, next_bunch + 4):
                        transpose_tile(j)
            elif i % BUNCH == bunch_at and next_bunch < N_TILES:
                for j in range(next_bunch, next_bunch + BUNCH):
                    transpose_tile(j)
            rotate_tile(i, *banks)
            if i + AHEAD < BY_TILE:
                quantise_tile(i + AHEAD)
            elif i + AHEAD - BY_TILE < ROWS // PAIR:
                quantise_pair(i + AHEAD - BY_TILE)
            if r == ROWS - 1:
                store_chunk(c)
        last_rotated(N_CHUNKS - 1)
